import numpy as np
import ml_dtypes


def mxq(x, axis, fmt="e4m3"):
    dtype, down = {"e4m3": (ml_dtypes.float8_e4m3fn, 7), "e5m2": (ml_dtypes.float8_e5m2, 14)}[fmt]
    v = np.moveaxis(np.asarray(x, np.float32).astype(ml_dtypes.bfloat16).astype(np.float64), axis, -1)
    blocks = v.reshape(v.shape[:-1] + (-1, 32))
    amax = np.abs(blocks).max(-1, keepdims=True)
    byte = np.maximum(np.where(amax > 0, np.frexp(amax)[1] - 1 + 127, 0) - down, 1)
    scale = np.exp2(byte - 127.0)
    codes = (blocks / scale).astype(np.float32).astype(dtype).astype(np.float64)
    return np.moveaxis((codes * scale).reshape(v.shape), -1, axis)


WIDE = False


def mx_kscale(k):
    if not WIDE:
        return np.ones(k)
    levels = np.array([10, -10, 5, -5, 0])
    a = np.random.permutation(np.resize(levels, k // 512 * 4)).reshape(k // 512, 4)
    idx = np.arange(k)
    return np.exp2(a[idx // 512, idx % 128 // 32])


BF16 = ml_dtypes.bfloat16


def bf(x):
    return np.asarray(x, np.float32).astype(BF16)


def f64(x):
    return np.asarray(x).astype(np.float64)


B, N, DIM, H, KD, D = 32, 256, 256, 4, 64, 128
DH = H * D
EPS = 1e-5


def hard_swish(v):
    return v * (np.minimum(np.maximum(v + 3.0, 0.0), 6.0) / 6.0)


def setup_inputs():
    t = mx_kscale(DH)
    c = 2.0 ** (-8.0 * np.random.random(DIM))
    return {"h_attn": bf(1.5 * np.random.standard_normal((B, N, DH)) * t),
            "proj_w": bf(np.random.standard_normal((DIM, DH)) * c[:, None] / np.sqrt(DH) / t),
            "proj_g": bf(1.0 + 0.1 * np.random.standard_normal(DIM)),
            "proj_b": bf(0.1 * np.random.standard_normal(DIM))}


def bn(y, g, b):
    m = y.mean(axis=(0, 1))
    v = ((y - m) ** 2).mean(axis=(0, 1))
    return (y - m) * (g / np.sqrt(v + EPS)) + b


def reference(h_attn, proj_w, proj_g, proj_b):
    h = hard_swish(f64(h_attn))
    y = mxq(h, 2, "e4m3") @ mxq(f64(proj_w), 1, "e4m3").T
    return bn(y, f64(proj_g), f64(proj_b))

@@ -1,0 +1,249 @@
+import concourse.mybir as mybir
+from concourse.masks import make_identity
+
+FP8X4 = mybir.dt.float8_e4m3fn_x4
+BF16 = mybir.dt.bfloat16
+F32 = mybir.dt.float32
+U32 = mybir.dt.uint32
+U8 = mybir.dt.uint8
+ACT = mybir.ActivationFunctionType
+ALU = mybir.AluOpType
+X_AXIS = mybir.AxisListType.X
+
+P = 128
+PACK = 4
+K = P * PACK
+ROWS = 32 * 256
+FEATURES = 256
+HALVES = FEATURES // P
+CHUNK = 512
+CHUNKS = ROWS // CHUNK
+BLOCKS = CHUNK // P
+PAIR = 2
+EPS = 1e-5
+
+FLOPS = 2 * ROWS * K * FEATURES
+
+
+def tile_attention_pb_t_kernel(tc, h_attn, proj_w, proj_g, proj_b, out):
+    nc = tc.nc
+
+    x_chunks = h_attn.flatten_outer_dims().rearrange("(i p j) k -> i p j k", p=P, j=BLOCKS)
+    out_chunks = out.flatten_outer_dims().rearrange("(i p j) c -> i p j c", p=P, j=BLOCKS)
+
+    with tc.tile_pool(name="keep", bufs=1) as keep, tc.tile_pool(
+        name="loads", bufs=CHUNKS
+    ) as loads, tc.tile_pool(name="stage", bufs=3) as stage:
+        w_rows = keep.tile([P, HALVES, K], BF16)
+        nc.sync.dma_start(out=w_rows[:], in_=proj_w.rearrange("(h c) k -> c h k", h=HALVES))
+        gb_rows = keep.tile([P, P], BF16)
+        nc.vector.memset(gb_rows[:], 0.0)
+        nc.sync.dma_start(
+            out=gb_rows[0:HALVES, :], in_=proj_g.rearrange("(h c) -> h c", h=HALVES)
+        )
+        nc.sync.dma_start(
+            out=gb_rows[HALVES : 2 * HALVES, :], in_=proj_b.rearrange("(h c) -> h c", h=HALVES)
+        )
+        x_tiles = []
+        for chunk in range(CHUNKS):
+            x_rows = loads.tile([P, BLOCKS, K], BF16, name="x_rows")
+            nc.sync.dma_start(out=x_rows[:], in_=x_chunks[chunk])
+            x_tiles.append(x_rows)
+
+        ident_bf16 = keep.tile([P, P], BF16)
+        make_identity(nc, ident_bf16[:])
+        ident_f32 = keep.tile([P, P], F32)
+        make_identity(nc, ident_f32[:])
+
+        one = keep.tile([P, 1], F32)
+        nc.vector.memset(one[:], 1.0)
+        nc.scalar.activation(out=one[:], in_=one[:], func=ACT.Sqrt)
+
+        w_codes = keep.tile([P, FEATURES], U32, align_bytes=64)
+        w_scales = keep.tile([P, FEATURES], U8, align_bytes=64)
+        h_codes = keep.tile([P, ROWS], U32, align_bytes=64)
+        h_scales = keep.tile([P, ROWS], U8, align_bytes=64)
+
+        def multiply(acc, half, chunk, start, stop):
+            features = slice(half * P, (half + 1) * P)
+            rows = slice(chunk * CHUNK, (chunk + 1) * CHUNK)
+            nc.tensor.matmul_mx(
+                out=acc,
+                lhsT=w_codes[:, features].bitcast(FP8X4),
+                lhsT_scale=w_scales[:, features],
+                rhs=h_codes[:, rows].bitcast(FP8X4),
+                rhs_scale=h_scales[:, rows],
+                start=start,
+                stop=stop,
+            )
+
+        gb = keep.tile([P, 2 * HALVES], F32)
+        neg_pivot = keep.tile([P, HALVES], F32)
+        sq_parts = keep.tile([P, HALVES, CHUNKS], F32)
+        gain = keep.tile([P, HALVES], F32)
+        shift = keep.tile([P, HALVES], F32)
+
+        with tc.psum_pool(name="psum_t", bufs=4) as psum_t, tc.psum_pool(
+            name="psum_y", bufs=2
+        ) as psum_y, tc.psum_pool(name="psum_sum", bufs=1) as psum_sum:
+            wT = psum_t.tile([P, PACK, FEATURES], BF16, tag="xT")
+            for half in range(HALVES):
+                for t in range(PACK):
+                    nc.tensor.transpose(
+                        wT[:, t, half * P : (half + 1) * P],
+                        w_rows[:, half, t * P : (t + 1) * P],
+                        ident_bf16[:],
+                    )
+            w_grouped = keep.tile([P, FEATURES, PACK], BF16, align_bytes=64)
+            nc.vector.tensor_copy(out=w_grouped[:], in_=wT[:].rearrange("q t c -> q c t"))
+            nc.vector.quantize_mx(
+                out=w_codes[:].bitcast(FP8X4),
+                scales=w_scales[:],
+                in_=w_grouped[:].rearrange("q c t -> q (c t)"),
+            )
+
+            gbT = psum_t.tile([P, P], BF16, tag="xT")
+            nc.tensor.transpose(gbT[:], gb_rows[:], ident_bf16[:])
+            nc.vector.tensor_copy(out=gb[:], in_=gbT[:, 0 : 2 * HALVES])
+
+            row_sums = [
+                psum_sum.tile([P, CHUNK], F32, name="row_sums%d" % half) for half in range(HALVES)
+            ]
+
+            for chunk in range(CHUNKS):
+                x_rows = x_tiles[chunk]
+                grouped = stage.tile([P, CHUNK, PACK], BF16, align_bytes=64)
+                for pair in range(BLOCKS // PAIR):
+                    xT = psum_t.tile([P, PACK, PAIR * P], BF16, tag="xT")
+                    for s in range(PAIR):
+                        for t in range(PACK):
+                            nc.tensor.transpose(
+                                xT[:, t, s * P : (s + 1) * P],
+                                x_rows[:, pair * PAIR + s, t * P : (t + 1) * P],
+                                ident_bf16[:],
+                            )
+                    x_by_row = xT[:].rearrange("q t r -> q r t")
+                    ramp = stage.tile([P, PAIR * P, PACK], F32)
+                    nc.scalar.activation(
+                        out=ramp[:], in_=x_by_row, func=ACT.Relu, scale=1.0 / 6.0, bias=0.5
+                    )
+                    nc.vector.scalar_tensor_tensor(
+                        out=grouped[:, pair * PAIR * P : (pair + 1) * PAIR * P, :],
+                        in0=ramp[:],
+                        scalar=1.0,
+                        in1=x_by_row,
+                        op0=ALU.min,
+                        op1=ALU.mult,
+                    )
+                rows = slice(chunk * CHUNK, (chunk + 1) * CHUNK)
+                nc.vector.quantize_mx(
+                    out=h_codes[:, rows].bitcast(FP8X4),
+                    scales=h_scales[:, rows],
+                    in_=grouped[:].rearrange("q r t -> q (r t)"),
+                )
+
+                y_banks = []
+                for half in range(HALVES):
+                    y = psum_y.tile([P, CHUNK], F32, name="y")
+                    multiply(y[:], half, chunk, True, True)
+                    multiply(row_sums[half][:], half, chunk, chunk == 0, chunk == CHUNKS - 1)
+                    y_banks.append(y)
+                if chunk == 0:
+                    first_sum = keep.tile([P, HALVES], F32)
+                    for half in range(HALVES):
+                        nc.vector.tensor_reduce(
+                            out=first_sum[:, half : half + 1],
+                            in_=y_banks[half][:],
+                            axis=X_AXIS,
+                            op=ALU.add,
+                        )
+                    nc.vector.tensor_scalar_mul(neg_pivot[:], first_sum[:], -1.0 / CHUNK)
+                for half in range(HALVES):
+                    squares = stage.tile([P, CHUNK], BF16)
+                    nc.scalar.activation(
+                        out=squares[:],
+                        in_=y_banks[half][:],
+                        func=ACT.Square,
+                        bias=neg_pivot[:, half : half + 1],
+                        accum_out=sq_parts[:, half, chunk : chunk + 1],
+                    )
+
+            total = keep.tile([P, HALVES], F32)
+            for half in range(HALVES):
+                nc.vector.tensor_reduce(
+                    out=total[:, half : half + 1], in_=row_sums[half][:], axis=X_AXIS, op=ALU.add
+                )
+            sq_total = keep.tile([P, HALVES], F32)
+            nc.vector.tensor_reduce(out=sq_total[:], in_=sq_parts[:], axis=X_AXIS, op=ALU.add)
+            mean = keep.tile([P, HALVES], F32)
+            nc.vector.tensor_scalar_mul(mean[:], total[:], 1.0 / ROWS)
+            off = keep.tile([P, HALVES], F32)
+            nc.vector.tensor_add(out=off[:], in0=mean[:], in1=neg_pivot[:])
+            off_sq = keep.tile([P, HALVES], F32)
+            nc.vector.tensor_mul(out=off_sq[:], in0=off[:], in1=off[:])
+            var = keep.tile([P, HALVES], F32)
+            nc.vector.scalar_tensor_tensor(
+                out=var[:],
+                in0=sq_total[:],
+                scalar=1.0 / ROWS,
+                in1=off_sq[:],
+                op0=ALU.mult,
+                op1=ALU.subtract,
+            )
+            var_eps = keep.tile([P, HALVES], F32)
+            nc.vector.tensor_scalar(
+                out=var_eps[:], in0=var[:], scalar1=0.0, scalar2=EPS, op0=ALU.max, op1=ALU.add
+            )
+            std = keep.tile([P, HALVES], F32)
+            nc.scalar.activation(out=std[:], in_=var_eps[:], func=ACT.Sqrt)
+            rstd = keep.tile([P, HALVES], F32)
+            nc.vector.reciprocal(out=rstd[:], in_=std[:])
+            nc.vector.tensor_mul(out=gain[:], in0=gb[:, 0:HALVES], in1=rstd[:])
+            mean_gain = keep.tile([P, HALVES], F32)
+            nc.vector.tensor_mul(out=mean_gain[:], in0=mean[:], in1=gain[:])
+            nc.vector.tensor_sub(out=shift[:], in0=gb[:, HALVES : 2 * HALVES], in1=mean_gain[:])
+
+        with tc.psum_pool(name="psum_y2", bufs=4, reuse_waits="tile") as psum_y2, tc.psum_pool(
+            name="psum_o", bufs=4, reuse_waits="tile"
+        ) as psum_o:
+            for chunk in range(CHUNKS):
+                y0 = psum_y2.tile([P, CHUNK], F32, tag="y2")
+                multiply(y0[:], 0, chunk, True, True)
+                normed0 = stage.tile([P, CHUNK], F32)
+                nc.scalar.activation(
+                    out=normed0[:],
+                    in_=y0[:],
+                    func=ACT.Identity,
+                    scale=gain[:, 0:1],
+                    bias=shift[:, 0:1],
+                )
+                y1 = psum_y2.tile([P, CHUNK], F32, tag="y2")
+                multiply(y1[:], 1, chunk, True, True)
+                normed1 = stage.tile([P, CHUNK], F32)
+                nc.vector.tensor_scalar(
+                    out=normed1[:],
+                    in0=y1[:],
+                    scalar1=gain[:, 1:2],
+                    scalar2=shift[:, 1:2],
+                    op0=ALU.mult,
+                    op1=ALU.add,
+                )
+                normed = [normed0, normed1]
+
+                result = stage.tile([P, BLOCKS, FEATURES], F32)
+                for pair in range(BLOCKS // PAIR):
+                    oT = psum_o.tile([P, PAIR, FEATURES], F32)
+                    for s in range(PAIR):
+                        block = pair * PAIR + s
+                        for half in range(HALVES):
+                            nc.tensor.transpose(
+                                oT[:, s, half * P : (half + 1) * P],
+                                normed[half][:, block * P : (block + 1) * P],
+                                ident_f32[:],
+                            )
+                    blocks = slice(pair * PAIR, (pair + 1) * PAIR)
+                    if pair == 0:
+                        nc.scalar.copy(out=result[:, blocks, :], in_=oT[:])
+                    else:
+                        nc.vector.tensor_copy(out=result[:, blocks, :], in_=oT[:])
+                nc.sync.dma_start(out=out_chunks[chunk], in_=result[:])

@@ -31,7 +31,7 @@ def tile_attention_pb_t_kernel(tc, h_attn, proj_w, proj_g, proj_b, out):
     x_chunks = h_attn.flatten_outer_dims().rearrange("(i p j) k -> i p j k", p=P, j=BLOCKS)
     out_chunks = out.flatten_outer_dims().rearrange("(i p j) c -> i p j c", p=P, j=BLOCKS)
 
-    with tc.tile_pool(name="keep", bufs=1) as keep, tc.tile_pool(
+    with tc.manual_schedule(), tc.tile_pool(name="keep", bufs=1) as keep, tc.tile_pool(
         name="loads", bufs=CHUNKS
     ) as loads, tc.tile_pool(name="stage", bufs=3) as stage:
         w_rows = keep.tile([P, HALVES, K], BF16)
@@ -86,7 +86,7 @@ def tile_attention_pb_t_kernel(tc, h_attn, proj_w, proj_g, proj_b, out):
         with tc.psum_pool(name="psum_t", bufs=4) as psum_t, tc.psum_pool(
             name="psum_y", bufs=2
         ) as psum_y, tc.psum_pool(name="psum_sum", bufs=1) as psum_sum:
-            wT = psum_t.tile([P, PACK, FEATURES], BF16, tag="xT")
+            wT = psum_y.tile([P, PACK, FEATURES], BF16, tag="y")
             for half in range(HALVES):
                 for t in range(PACK):
                     nc.tensor.transpose(
@@ -102,27 +102,32 @@ def tile_attention_pb_t_kernel(tc, h_attn, proj_w, proj_g, proj_b, out):
                 in_=w_grouped[:].rearrange("q c t -> q (c t)"),
             )
 
-            gbT = psum_t.tile([P, P], BF16, tag="xT")
+            gbT = psum_y.tile([P, P], BF16, tag="y")
             nc.tensor.transpose(gbT[:], gb_rows[:], ident_bf16[:])
             nc.vector.tensor_copy(out=gb[:], in_=gbT[:, 0 : 2 * HALVES])
 
             row_sums = [
                 psum_sum.tile([P, CHUNK], F32, name="row_sums%d" % half) for half in range(HALVES)
             ]
+            xT_banks = {}
+            y_banks = {}
 
-            for chunk in range(CHUNKS):
-                x_rows = x_tiles[chunk]
-                grouped = stage.tile([P, CHUNK, PACK], BF16, align_bytes=64)
+            def transposes(chunk):
                 for pair in range(BLOCKS // PAIR):
-                    xT = psum_t.tile([P, PACK, PAIR * P], BF16, tag="xT")
+                    xT = psum_t.tile([P, PACK, PAIR * P], BF16, name="xT")
                     for s in range(PAIR):
                         for t in range(PACK):
                             nc.tensor.transpose(
                                 xT[:, t, s * P : (s + 1) * P],
-                                x_rows[:, pair * PAIR + s, t * P : (t + 1) * P],
+                                x_tiles[chunk][:, pair * PAIR + s, t * P : (t + 1) * P],
                                 ident_bf16[:],
                             )
-                    x_by_row = xT[:].rearrange("q t r -> q r t")
+                    xT_banks[(chunk, pair)] = xT
+
+            def swish_and_quantise(chunk):
+                grouped = stage.tile([P, CHUNK, PACK], BF16, align_bytes=64)
+                for pair in range(BLOCKS // PAIR):
+                    x_by_row = xT_banks[(chunk, pair)][:].rearrange("q t r -> q r t")
                     ramp = stage.tile([P, PAIR * P, PACK], F32)
                     nc.scalar.activation(
                         out=ramp[:], in_=x_by_row, func=ACT.Relu, scale=1.0 / 6.0, bias=0.5
@@ -142,31 +147,48 @@ def tile_attention_pb_t_kernel(tc, h_attn, proj_w, proj_g, proj_b, out):
                     in_=grouped[:].rearrange("q r t -> q (r t)"),
                 )
 
-                y_banks = []
+            def products(chunk):
                 for half in range(HALVES):
                     y = psum_y.tile([P, CHUNK], F32, name="y")
                     multiply(y[:], half, chunk, True, True)
                     multiply(row_sums[half][:], half, chunk, chunk == 0, chunk == CHUNKS - 1)
-                    y_banks.append(y)
-                if chunk == 0:
-                    first_sum = keep.tile([P, HALVES], F32)
-                    for half in range(HALVES):
-                        nc.vector.tensor_reduce(
-                            out=first_sum[:, half : half + 1],
-                            in_=y_banks[half][:],
-                            axis=X_AXIS,
-                            op=ALU.add,
-                        )
-                    nc.vector.tensor_scalar_mul(neg_pivot[:], first_sum[:], -1.0 / CHUNK)
+                    y_banks[(chunk, half)] = y
+
+            def choose_pivot():
+                first_sum = keep.tile([P, HALVES], F32)
                 for half in range(HALVES):
-                    squares = stage.tile([P, CHUNK], BF16)
+                    nc.vector.tensor_reduce(
+                        out=first_sum[:, half : half + 1],
+                        in_=y_banks[(0, half)][:, 0:P],
+                        axis=X_AXIS,
+                        op=ALU.add,
+                    )
+                nc.vector.tensor_scalar_mul(neg_pivot[:], first_sum[:], -1.0 / P)
+
+            def squares(chunk):
+                for half in range(HALVES):
+                    unread = stage.tile([P, CHUNK], BF16)
                     nc.scalar.activation(
-                        out=squares[:],
-                        in_=y_banks[half][:],
+                        out=unread[:],
+                        in_=y_banks[(chunk, half)][:],
                         func=ACT.Square,
                         bias=neg_pivot[:, half : half + 1],
                         accum_out=sq_parts[:, half, chunk : chunk + 1],
                     )
+
+            transposes(0)
+            transposes(1)
+            for step in range(CHUNKS + 2):
+                if 1 <= step <= CHUNKS:
+                    products(step - 1)
+                if step == 1:
+                    choose_pivot()
+                if step < CHUNKS:
+                    swish_and_quantise(step)
+                if step >= 2:
+                    squares(step - 2)
+                if step + 2 < CHUNKS:
+                    transposes(step + 2)
 
             total = keep.tile([P, HALVES], F32)
             for half in range(HALVES):
@@ -206,30 +228,37 @@ def tile_attention_pb_t_kernel(tc, h_attn, proj_w, proj_g, proj_b, out):
         with tc.psum_pool(name="psum_y2", bufs=4, reuse_waits="tile") as psum_y2, tc.psum_pool(
             name="psum_o", bufs=4, reuse_waits="tile"
         ) as psum_o:
-            for chunk in range(CHUNKS):
-                y0 = psum_y2.tile([P, CHUNK], F32, tag="y2")
-                multiply(y0[:], 0, chunk, True, True)
+            y2_banks = {}
+            normed = {}
+
+            def products_again(chunk):
+                for half in range(HALVES):
+                    y2 = psum_y2.tile([P, CHUNK], F32, name="y2")
+                    multiply(y2[:], half, chunk, True, True)
+                    y2_banks[(chunk, half)] = y2
+
+            def normalise(chunk):
                 normed0 = stage.tile([P, CHUNK], F32)
                 nc.scalar.activation(
                     out=normed0[:],
-                    in_=y0[:],
+                    in_=y2_banks[(chunk, 0)][:],
                     func=ACT.Identity,
                     scale=gain[:, 0:1],
                     bias=shift[:, 0:1],
                 )
-                y1 = psum_y2.tile([P, CHUNK], F32, tag="y2")
-                multiply(y1[:], 1, chunk, True, True)
                 normed1 = stage.tile([P, CHUNK], F32)
                 nc.vector.tensor_scalar(
                     out=normed1[:],
-                    in0=y1[:],
+                    in0=y2_banks[(chunk, 1)][:],
                     scalar1=gain[:, 1:2],
                     scalar2=shift[:, 1:2],
                     op0=ALU.mult,
                     op1=ALU.add,
                 )
-                normed = [normed0, normed1]
+                normed[(chunk, 0)] = normed0
+                normed[(chunk, 1)] = normed1
 
+            def transpose_back_and_store(chunk):
                 result = stage.tile([P, BLOCKS, FEATURES], F32)
                 for pair in range(BLOCKS // PAIR):
                     oT = psum_o.tile([P, PAIR, FEATURES], F32)
@@ -238,7 +267,7 @@ def tile_attention_pb_t_kernel(tc, h_attn, proj_w, proj_g, proj_b, out):
                         for half in range(HALVES):
                             nc.tensor.transpose(
                                 oT[:, s, half * P : (half + 1) * P],
-                                normed[half][:, block * P : (block + 1) * P],
+                                normed[(chunk, half)][:, block * P : (block + 1) * P],
                                 ident_f32[:],
                             )
                     blocks = slice(pair * PAIR, (pair + 1) * PAIR)
@@ -247,3 +276,13 @@ def tile_attention_pb_t_kernel(tc, h_attn, proj_w, proj_g, proj_b, out):
                     else:
                         nc.vector.tensor_copy(out=result[:, blocks, :], in_=oT[:])
                 nc.sync.dma_start(out=out_chunks[chunk], in_=result[:])
+
+            products_again(0)
+            products_again(1)
+            normalise(0)
+            for chunk in range(CHUNKS):
+                if chunk + 1 < CHUNKS:
+                    normalise(chunk + 1)
+                transpose_back_and_store(chunk)
+                if chunk + 2 < CHUNKS:
+                    products_again(chunk + 2)

@@ -20,6 +20,7 @@ CHUNK = 512
 CHUNKS = ROWS // CHUNK
 BLOCKS = CHUNK // P
 PAIR = 2
+PAIRS = BLOCKS // PAIR
 EPS = 1e-5
 
 FLOPS = 2 * ROWS * K * FEATURES
@@ -32,7 +33,7 @@ def tile_attention_pb_t_kernel(tc, h_attn, proj_w, proj_g, proj_b, out):
     out_chunks = out.flatten_outer_dims().rearrange("(i p j) c -> i p j c", p=P, j=BLOCKS)
 
     with tc.manual_schedule(), tc.tile_pool(name="keep", bufs=1) as keep, tc.tile_pool(
-        name="loads", bufs=CHUNKS
+        name="loads", bufs=CHUNKS * PAIRS
     ) as loads, tc.tile_pool(name="stage", bufs=3) as stage:
         w_rows = keep.tile([P, HALVES, K], BF16)
         nc.sync.dma_start(out=w_rows[:], in_=proj_w.rearrange("(h c) k -> c h k", h=HALVES))
@@ -44,11 +45,14 @@ def tile_attention_pb_t_kernel(tc, h_attn, proj_w, proj_g, proj_b, out):
         nc.sync.dma_start(
             out=gb_rows[HALVES : 2 * HALVES, :], in_=proj_b.rearrange("(h c) -> h c", h=HALVES)
         )
-        x_tiles = []
+        x_tiles = {}
         for chunk in range(CHUNKS):
-            x_rows = loads.tile([P, BLOCKS, K], BF16, name="x_rows")
-            nc.sync.dma_start(out=x_rows[:], in_=x_chunks[chunk])
-            x_tiles.append(x_rows)
+            for pair in range(PAIRS):
+                x_rows = loads.tile([P, PAIR, K], BF16, name="x_rows")
+                nc.sync.dma_start(
+                    out=x_rows[:], in_=x_chunks[chunk][:, pair * PAIR : (pair + 1) * PAIR, :]
+                )
+                x_tiles[(chunk, pair)] = x_rows
 
         ident_bf16 = keep.tile([P, P], BF16)
         make_identity(nc, ident_bf16[:])
@@ -110,41 +114,46 @@ def tile_attention_pb_t_kernel(tc, h_attn, proj_w, proj_g, proj_b, out):
                 psum_sum.tile([P, CHUNK], F32, name="row_sums%d" % half) for half in range(HALVES)
             ]
             xT_banks = {}
+            grouped_tiles = {}
             y_banks = {}
 
             def transposes(chunk):
-                for pair in range(BLOCKS // PAIR):
+                for pair in range(PAIRS):
                     xT = psum_t.tile([P, PACK, PAIR * P], BF16, name="xT")
                     for s in range(PAIR):
                         for t in range(PACK):
                             nc.tensor.transpose(
                                 xT[:, t, s * P : (s + 1) * P],
-                                x_tiles[chunk][:, pair * PAIR + s, t * P : (t + 1) * P],
+                                x_tiles[(chunk, pair)][:, s, t * P : (t + 1) * P],
                                 ident_bf16[:],
                             )
                     xT_banks[(chunk, pair)] = xT
 
-            def swish_and_quantise(chunk):
-                grouped = stage.tile([P, CHUNK, PACK], BF16, align_bytes=64)
-                for pair in range(BLOCKS // PAIR):
-                    x_by_row = xT_banks[(chunk, pair)][:].rearrange("q t r -> q r t")
-                    ramp = stage.tile([P, PAIR * P, PACK], F32)
-                    nc.scalar.activation(
-                        out=ramp[:], in_=x_by_row, func=ACT.Relu, scale=1.0 / 6.0, bias=0.5
+            def swish(chunk, pair):
+                if pair == 0:
+                    grouped_tiles[chunk] = stage.tile(
+                        [P, CHUNK, PACK], BF16, align_bytes=64, name="grouped"
                     )
-                    nc.vector.scalar_tensor_tensor(
-                        out=grouped[:, pair * PAIR * P : (pair + 1) * PAIR * P, :],
-                        in0=ramp[:],
-                        scalar=1.0,
-                        in1=x_by_row,
-                        op0=ALU.min,
-                        op1=ALU.mult,
-                    )
+                x_by_row = xT_banks[(chunk, pair)][:].rearrange("q t r -> q r t")
+                ramp = stage.tile([P, PAIR * P, PACK], F32)
+                nc.scalar.activation(
+                    out=ramp[:], in_=x_by_row, func=ACT.Relu, scale=1.0 / 6.0, bias=0.5
+                )
+                nc.vector.scalar_tensor_tensor(
+                    out=grouped_tiles[chunk][:, pair * PAIR * P : (pair + 1) * PAIR * P, :],
+                    in0=ramp[:],
+                    scalar=1.0,
+                    in1=x_by_row,
+                    op0=ALU.min,
+                    op1=ALU.mult,
+                )
+
+            def quantise(chunk):
                 rows = slice(chunk * CHUNK, (chunk + 1) * CHUNK)
                 nc.vector.quantize_mx(
                     out=h_codes[:, rows].bitcast(FP8X4),
                     scales=h_scales[:, rows],
-                    in_=grouped[:].rearrange("q r t -> q (r t)"),
+                    in_=grouped_tiles[chunk][:].rearrange("q r t -> q (r t)"),
                 )
 
             def products(chunk):
@@ -178,15 +187,19 @@ def tile_attention_pb_t_kernel(tc, h_attn, proj_w, proj_g, proj_b, out):
 
             transposes(0)
             transposes(1)
-            for step in range(CHUNKS + 2):
-                if 1 <= step <= CHUNKS:
-                    products(step - 1)
-                if step == 1:
+            for step in range(CHUNKS + 3):
+                if 2 <= step < CHUNKS + 2:
+                    products(step - 2)
+                if step == 2:
                     choose_pivot()
                 if step < CHUNKS:
-                    swish_and_quantise(step)
-                if step >= 2:
-                    squares(step - 2)
+                    swish(step, 0)
+                if 1 <= step <= CHUNKS:
+                    quantise(step - 1)
+                if step < CHUNKS:
+                    swish(step, 1)
+                if step >= 3:
+                    squares(step - 3)
                 if step + 2 < CHUNKS:
                     transposes(step + 2)
 
@@ -195,14 +208,14 @@ def tile_attention_pb_t_kernel(tc, h_attn, proj_w, proj_g, proj_b, out):
                 nc.vector.tensor_reduce(
                     out=total[:, half : half + 1], in_=row_sums[half][:], axis=X_AXIS, op=ALU.add
                 )
-            sq_total = keep.tile([P, HALVES], F32)
-            nc.vector.tensor_reduce(out=sq_total[:], in_=sq_parts[:], axis=X_AXIS, op=ALU.add)
             mean = keep.tile([P, HALVES], F32)
             nc.vector.tensor_scalar_mul(mean[:], total[:], 1.0 / ROWS)
             off = keep.tile([P, HALVES], F32)
             nc.vector.tensor_add(out=off[:], in0=mean[:], in1=neg_pivot[:])
             off_sq = keep.tile([P, HALVES], F32)
             nc.vector.tensor_mul(out=off_sq[:], in0=off[:], in1=off[:])
+            sq_total = keep.tile([P, HALVES], F32)
+            nc.vector.tensor_reduce(out=sq_total[:], in_=sq_parts[:], axis=X_AXIS, op=ALU.add)
             var = keep.tile([P, HALVES], F32)
             nc.vector.scalar_tensor_tensor(
                 out=var[:],
@@ -260,7 +273,7 @@ def tile_attention_pb_t_kernel(tc, h_attn, proj_w, proj_g, proj_b, out):
 
             def transpose_back_and_store(chunk):
                 result = stage.tile([P, BLOCKS, FEATURES], F32)
-                for pair in range(BLOCKS // PAIR):
+                for pair in range(PAIRS):
                     oT = psum_o.tile([P, PAIR, FEATURES], F32)
                     for s in range(PAIR):
                         block = pair * PAIR + s
@@ -275,7 +288,7 @@ def tile_attention_pb_t_kernel(tc, h_attn, proj_w, proj_g, proj_b, out):
                         nc.scalar.copy(out=result[:, blocks, :], in_=oT[:])
                     else:
                         nc.vector.tensor_copy(out=result[:, blocks, :], in_=oT[:])
-                nc.sync.dma_start(out=out_chunks[chunk], in_=result[:])
+                    nc.sync.dma_start(out=out_chunks[chunk][:, blocks, :], in_=result[:, blocks, :])
 
             products_again(0)
             products_again(1)

import concourse.mybir as mybir
from concourse.masks import make_identity

FP8X4 = mybir.dt.float8_e4m3fn_x4
BF16 = mybir.dt.bfloat16
F32 = mybir.dt.float32
U32 = mybir.dt.uint32
U8 = mybir.dt.uint8
ACT = mybir.ActivationFunctionType
ALU = mybir.AluOpType
X_AXIS = mybir.AxisListType.X

P = 128
PACK = 4
K = P * PACK
ROWS = 32 * 256
FEATURES = 256
HALVES = FEATURES // P
CHUNK = 512
CHUNKS = ROWS // CHUNK
BLOCKS = CHUNK // P
PAIR = 2
PAIRS = BLOCKS // PAIR
EPS = 1e-5

FLOPS = 2 * ROWS * K * FEATURES


def tile_attention_pb_t_kernel(tc, h_attn, proj_w, proj_g, proj_b, out):
    nc = tc.nc

    x_chunks = h_attn.flatten_outer_dims().rearrange("(i p j) k -> i p j k", p=P, j=BLOCKS)
    out_chunks = out.flatten_outer_dims().rearrange("(i p j) c -> i p j c", p=P, j=BLOCKS)

    with tc.manual_schedule(), tc.tile_pool(name="keep", bufs=1) as keep, tc.tile_pool(
        name="loads", bufs=CHUNKS * PAIRS
    ) as loads, tc.tile_pool(name="stage", bufs=3) as stage:
        w_rows = keep.tile([P, HALVES, K], BF16)
        nc.sync.dma_start(out=w_rows[:], in_=proj_w.rearrange("(h c) k -> c h k", h=HALVES))
        gb_rows = keep.tile([P, P], BF16)
        nc.vector.memset(gb_rows[:], 0.0)
        nc.sync.dma_start(
            out=gb_rows[0:HALVES, :], in_=proj_g.rearrange("(h c) -> h c", h=HALVES)
        )
        nc.sync.dma_start(
            out=gb_rows[HALVES : 2 * HALVES, :], in_=proj_b.rearrange("(h c) -> h c", h=HALVES)
        )
        x_tiles = {}
        for chunk in range(CHUNKS):
            for pair in range(PAIRS):
                x_rows = loads.tile([P, PAIR, K], BF16, name="x_rows")
                nc.sync.dma_start(
                    out=x_rows[:], in_=x_chunks[chunk][:, pair * PAIR : (pair + 1) * PAIR, :]
                )
                x_tiles[(chunk, pair)] = x_rows

        ident_bf16 = keep.tile([P, P], BF16)
        make_identity(nc, ident_bf16[:])
        ident_f32 = keep.tile([P, P], F32)
        make_identity(nc, ident_f32[:])

        one = keep.tile([P, 1], F32)
        nc.vector.memset(one[:], 1.0)
        nc.scalar.activation(out=one[:], in_=one[:], func=ACT.Sqrt)

        w_codes = keep.tile([P, FEATURES], U32, align_bytes=64)
        w_scales = keep.tile([P, FEATURES], U8, align_bytes=64)
        h_codes = keep.tile([P, ROWS], U32, align_bytes=64)
        h_scales = keep.tile([P, ROWS], U8, align_bytes=64)

        def multiply(acc, half, chunk, start, stop):
            features = slice(half * P, (half + 1) * P)
            rows = slice(chunk * CHUNK, (chunk + 1) * CHUNK)
            nc.tensor.matmul_mx(
                out=acc,
                lhsT=w_codes[:, features].bitcast(FP8X4),
                lhsT_scale=w_scales[:, features],
                rhs=h_codes[:, rows].bitcast(FP8X4),
                rhs_scale=h_scales[:, rows],
                start=start,
                stop=stop,
            )

        gb = keep.tile([P, 2 * HALVES], F32)
        neg_pivot = keep.tile([P, HALVES], F32)
        sq_parts = keep.tile([P, HALVES, CHUNKS], F32)
        gain = keep.tile([P, HALVES], F32)
        shift = keep.tile([P, HALVES], F32)

        with tc.psum_pool(name="psum_t", bufs=4) as psum_t, tc.psum_pool(
            name="psum_y", bufs=2
        ) as psum_y, tc.psum_pool(name="psum_sum", bufs=1) as psum_sum:
            wT = psum_y.tile([P, PACK, FEATURES], BF16, tag="y")
            for half in range(HALVES):
                for t in range(PACK):
                    nc.tensor.transpose(
                        wT[:, t, half * P : (half + 1) * P],
                        w_rows[:, half, t * P : (t + 1) * P],
                        ident_bf16[:],
                    )
            w_grouped = keep.tile([P, FEATURES, PACK], BF16, align_bytes=64)
            nc.vector.tensor_copy(out=w_grouped[:], in_=wT[:].rearrange("q t c -> q c t"))
            nc.vector.quantize_mx(
                out=w_codes[:].bitcast(FP8X4),
                scales=w_scales[:],
                in_=w_grouped[:].rearrange("q c t -> q (c t)"),
            )

            gbT = psum_y.tile([P, P], BF16, tag="y")
            nc.tensor.transpose(gbT[:], gb_rows[:], ident_bf16[:])
            nc.vector.tensor_copy(out=gb[:], in_=gbT[:, 0 : 2 * HALVES])

            row_sums = [
                psum_sum.tile([P, CHUNK], F32, name="row_sums%d" % half) for half in range(HALVES)
            ]
            xT_banks = {}
            grouped_tiles = {}
            y_banks = {}

            def transposes(chunk):
                for pair in range(PAIRS):
                    xT = psum_t.tile([P, PACK, PAIR * P], BF16, name="xT")
                    for s in range(PAIR):
                        for t in range(PACK):
                            nc.tensor.transpose(
                                xT[:, t, s * P : (s + 1) * P],
                                x_tiles[(chunk, pair)][:, s, t * P : (t + 1) * P],
                                ident_bf16[:],
                            )
                    xT_banks[(chunk, pair)] = xT

            def swish(chunk, pair):
                if pair == 0:
                    grouped_tiles[chunk] = stage.tile(
                        [P, CHUNK, PACK], BF16, align_bytes=64, name="grouped"
                    )
                x_by_row = xT_banks[(chunk, pair)][:].rearrange("q t r -> q r t")
                ramp = stage.tile([P, PAIR * P, PACK], F32)
                nc.scalar.activation(
                    out=ramp[:], in_=x_by_row, func=ACT.Relu, scale=1.0 / 6.0, bias=0.5
                )
                nc.vector.scalar_tensor_tensor(
                    out=grouped_tiles[chunk][:, pair * PAIR * P : (pair + 1) * PAIR * P, :],
                    in0=ramp[:],
                    scalar=1.0,
                    in1=x_by_row,
                    op0=ALU.min,
                    op1=ALU.mult,
                )

            def quantise(chunk):
                rows = slice(chunk * CHUNK, (chunk + 1) * CHUNK)
                nc.vector.quantize_mx(
                    out=h_codes[:, rows].bitcast(FP8X4),
                    scales=h_scales[:, rows],
                    in_=grouped_tiles[chunk][:].rearrange("q r t -> q (r t)"),
                )

            def products(chunk):
                for half in range(HALVES):
                    y = psum_y.tile([P, CHUNK], F32, name="y")
                    multiply(y[:], half, chunk, True, True)
                    multiply(row_sums[half][:], half, chunk, chunk == 0, chunk == CHUNKS - 1)
                    y_banks[(chunk, half)] = y

            def choose_pivot():
                first_sum = keep.tile([P, HALVES], F32)
                for half in range(HALVES):
                    nc.vector.tensor_reduce(
                        out=first_sum[:, half : half + 1],
                        in_=y_banks[(0, half)][:, 0:P],
                        axis=X_AXIS,
                        op=ALU.add,
                    )
                nc.vector.tensor_scalar_mul(neg_pivot[:], first_sum[:], -1.0 / P)

            def squares(chunk):
                for half in range(HALVES):
                    unread = stage.tile([P, CHUNK], BF16)
                    nc.scalar.activation(
                        out=unread[:],
                        in_=y_banks[(chunk, half)][:],
                        func=ACT.Square,
                        bias=neg_pivot[:, half : half + 1],
                        accum_out=sq_parts[:, half, chunk : chunk + 1],
                    )

            transposes(0)
            transposes(1)
            for step in range(CHUNKS + 3):
                if 2 <= step < CHUNKS + 2:
                    products(step - 2)
                if step == 2:
                    choose_pivot()
                if step < CHUNKS:
                    swish(step, 0)
                if 1 <= step <= CHUNKS:
                    quantise(step - 1)
                if step < CHUNKS:
                    swish(step, 1)
                if step >= 3:
                    squares(step - 3)
                if step + 2 < CHUNKS:
                    transposes(step + 2)

            total = keep.tile([P, HALVES], F32)
            for half in range(HALVES):
                nc.vector.tensor_reduce(
                    out=total[:, half : half + 1], in_=row_sums[half][:], axis=X_AXIS, op=ALU.add
                )
            mean = keep.tile([P, HALVES], F32)
            nc.vector.tensor_scalar_mul(mean[:], total[:], 1.0 / ROWS)
            off = keep.tile([P, HALVES], F32)
            nc.vector.tensor_add(out=off[:], in0=mean[:], in1=neg_pivot[:])
            off_sq = keep.tile([P, HALVES], F32)
            nc.vector.tensor_mul(out=off_sq[:], in0=off[:], in1=off[:])
            sq_total = keep.tile([P, HALVES], F32)
            nc.vector.tensor_reduce(out=sq_total[:], in_=sq_parts[:], axis=X_AXIS, op=ALU.add)
            var = keep.tile([P, HALVES], F32)
            nc.vector.scalar_tensor_tensor(
                out=var[:],
                in0=sq_total[:],
                scalar=1.0 / ROWS,
                in1=off_sq[:],
                op0=ALU.mult,
                op1=ALU.subtract,
            )
            var_eps = keep.tile([P, HALVES], F32)
            nc.vector.tensor_scalar(
                out=var_eps[:], in0=var[:], scalar1=0.0, scalar2=EPS, op0=ALU.max, op1=ALU.add
            )
            std = keep.tile([P, HALVES], F32)
            nc.scalar.activation(out=std[:], in_=var_eps[:], func=ACT.Sqrt)
            rstd = keep.tile([P, HALVES], F32)
            nc.vector.reciprocal(out=rstd[:], in_=std[:])
            nc.vector.tensor_mul(out=gain[:], in0=gb[:, 0:HALVES], in1=rstd[:])
            mean_gain = keep.tile([P, HALVES], F32)
            nc.vector.tensor_mul(out=mean_gain[:], in0=mean[:], in1=gain[:])
            nc.vector.tensor_sub(out=shift[:], in0=gb[:, HALVES : 2 * HALVES], in1=mean_gain[:])

        with tc.psum_pool(name="psum_y2", bufs=4, reuse_waits="tile") as psum_y2, tc.psum_pool(
            name="psum_o", bufs=4, reuse_waits="tile"
        ) as psum_o:
            y2_banks = {}
            normed = {}

            def products_again(chunk):
                for half in range(HALVES):
                    y2 = psum_y2.tile([P, CHUNK], F32, name="y2")
                    multiply(y2[:], half, chunk, True, True)
                    y2_banks[(chunk, half)] = y2

            def normalise(chunk):
                normed0 = stage.tile([P, CHUNK], F32)
                nc.scalar.activation(
                    out=normed0[:],
                    in_=y2_banks[(chunk, 0)][:],
                    func=ACT.Identity,
                    scale=gain[:, 0:1],
                    bias=shift[:, 0:1],
                )
                normed1 = stage.tile([P, CHUNK], F32)
                nc.vector.tensor_scalar(
                    out=normed1[:],
                    in0=y2_banks[(chunk, 1)][:],
                    scalar1=gain[:, 1:2],
                    scalar2=shift[:, 1:2],
                    op0=ALU.mult,
                    op1=ALU.add,
                )
                normed[(chunk, 0)] = normed0
                normed[(chunk, 1)] = normed1

            def transpose_back_and_store(chunk):
                result = stage.tile([P, BLOCKS, FEATURES], F32)
                for pair in range(PAIRS):
                    oT = psum_o.tile([P, PAIR, FEATURES], F32)
                    for s in range(PAIR):
                        block = pair * PAIR + s
                        for half in range(HALVES):
                            nc.tensor.transpose(
                                oT[:, s, half * P : (half + 1) * P],
                                normed[(chunk, half)][:, block * P : (block + 1) * P],
                                ident_f32[:],
                            )
                    blocks = slice(pair * PAIR, (pair + 1) * PAIR)
                    if pair == 0:
                        nc.scalar.copy(out=result[:, blocks, :], in_=oT[:])
                    else:
                        nc.vector.tensor_copy(out=result[:, blocks, :], in_=oT[:])
                    nc.sync.dma_start(out=out_chunks[chunk][:, blocks, :], in_=result[:, blocks, :])

            products_again(0)
            products_again(1)
            normalise(0)
            for chunk in range(CHUNKS):
                if chunk + 1 < CHUNKS:
                    normalise(chunk + 1)
                transpose_back_and_store(chunk)
                if chunk + 2 < CHUNKS:
                    products_again(chunk + 2)
